import numpy as np
import ml_dtypes


def mxq(x, axis, fmt="e4m3"):
    dtype, down = {"e4m3": (ml_dtypes.float8_e4m3fn, 7), "e5m2": (ml_dtypes.float8_e5m2, 14)}[fmt]
    v = np.moveaxis(np.asarray(x, np.float32).astype(ml_dtypes.bfloat16).astype(np.float64), axis, -1)
    blocks = v.reshape(v.shape[:-1] + (-1, 32))
    amax = np.abs(blocks).max(-1, keepdims=True)
    byte = np.maximum(np.where(amax > 0, np.frexp(amax)[1] - 1 + 127, 0) - down, 1)
    scale = np.exp2(byte - 127.0)
    codes = (blocks / scale).astype(np.float32).astype(dtype).astype(np.float64)
    return np.moveaxis((codes * scale).reshape(v.shape), -1, axis)


WIDE = False


def mx_kscale(k):
    if not WIDE:
        return np.ones(k)
    levels = np.array([10, -10, 5, -5, 0])
    if k % 512:
        return np.exp2(np.random.permutation(np.resize(levels, k // 32))).repeat(32)
    a = np.empty((k // 512, 16))
    for p in range(k // 512):
        a[p, :8] = np.random.permutation(np.resize(levels, 8))
        for g in range(8):
            far = levels[np.abs(levels - a[p, g]) >= 10]
            a[p, g + 8] = far[np.random.randint(len(far))]
    return np.exp2(a.ravel()).repeat(32)


BF16 = ml_dtypes.bfloat16


def bf(x):
    return np.asarray(x, np.float32).astype(BF16)


def f64(x):
    return np.asarray(x).astype(np.float64)


N_FFT, B, T = 1024, 16, 128
STRIDE = N_FFT + 1
L = T * STRIDE


def _fourier_kernels(n_fft):
    s = np.arange(n_fft, dtype=np.float64)
    k = np.arange(n_fft, dtype=np.float64)[:, None]
    ang = 2.0 * np.pi * k * s / n_fft
    return np.sin(ang), np.cos(ang)


def setup_inputs():
    s = mx_kscale(N_FFT)
    sx = np.concatenate([s, np.ones(1)])
    x = (np.random.standard_normal((1, B, T, STRIDE)) * sx).reshape(1, B, L)
    ws, wc = _fourier_kernels(N_FFT)
    wsin = (ws + 0.5 * np.random.standard_normal((N_FFT, N_FFT))) / np.sqrt(N_FFT) / s[None, :]
    wcos = (wc + 0.5 * np.random.standard_normal((N_FFT, N_FFT))) / np.sqrt(N_FFT) / s[None, :]
    return {"x": bf(x), "wsin": bf(wsin), "wcos": bf(wcos)}


def reference(x, wsin, wcos):
    sig = f64(x)[0]
    frames = sig.reshape(B, T, STRIDE)[..., :N_FFT]
    fq = mxq(frames, 2, "e4m3")
    real = np.einsum('btn,kn->tbk', fq, mxq(f64(wcos), 1, "e4m3"))
    imag = np.einsum('btn,kn->tbk', fq, mxq(f64(wsin), 1, "e4m3"))
    return real, -imag

@@ -1,0 +1,196 @@
+from contextlib import ExitStack
+
+import concourse.mybir as mybir
+from concourse.masks import make_identity
+
+BF16 = mybir.dt.bfloat16
+F32 = mybir.dt.float32
+U32 = mybir.dt.uint32
+U8 = mybir.dt.uint8
+FP8X4 = mybir.dt.float8_e4m3fn_x4
+
+P = 128
+N_FFT = 1024
+SIGNALS = 16
+FRAMES = 128
+STRIDE = N_FFT + 1
+PACK = 4
+K_PASS = P * PACK
+PASSES = N_FFT // K_PASS
+PLANES = 2
+WORDS = K_PASS // 2
+N_TILE = 512
+COL_TILES = N_FFT // N_TILE
+PAIR = 2
+ROUNDS = SIGNALS // PAIR
+W_ROWS = PAIR * P
+W_CHUNKS = N_FFT // W_ROWS
+COS = 0
+SIN = 1
+
+FLOPS = 2 * 2 * SIGNALS * FRAMES * N_FFT * N_FFT
+
+
+def tile_dftlayer_kernel(tc, x, wsin, wcos, out_0, out_1):
+    nc = tc.nc
+    weights = {COS: wcos, SIN: wsin}
+    outputs = {COS: out_0, SIN: out_1}
+    signs = {COS: 1.0, SIN: -1.0}
+
+    with ExitStack() as ctx:
+        ctx.enter_context(tc.manual_schedule())
+        keep = ctx.enter_context(tc.tile_pool(name="keep", bufs=1))
+        stage = ctx.enter_context(tc.tile_pool(name="stage", bufs=4))
+        results = ctx.enter_context(tc.tile_pool(name="results", bufs=8))
+        psum_t = ctx.enter_context(tc.psum_pool(name="psum_t", bufs=4))
+        psum_acc = ctx.enter_context(tc.psum_pool(name="psum_acc", bufs=4))
+
+        ident = keep.tile([P, P], F32, name="ident")
+        make_identity(nc, ident[:])
+
+        x_frames = x.rearrange("o b (t s) -> t (o b) s", s=STRIDE)
+        x_raw = [keep.tile([P, PAIR, N_FFT], BF16, name="x_raw%d" % i) for i in range(ROUNDS)]
+        w_raw = {
+            (half, c): keep.tile([P, PAIR, N_FFT], BF16, name="w_raw%d_%d" % (half, c))
+            for half in (COS, SIN)
+            for c in range(W_CHUNKS)
+        }
+
+        def load_frames(i):
+            nc.sync.dma_start(out=x_raw[i][:], in_=x_frames[:, PAIR * i : PAIR * (i + 1), 0:N_FFT])
+
+        def load_weights(half):
+            rows = weights[half].rearrange("(c q r) n -> c q r n", q=P, r=PAIR)
+            for c in range(W_CHUNKS):
+                nc.sync.dma_start(out=w_raw[(half, c)][:], in_=rows[c, :, :, :])
+
+        load_frames(0)
+        load_weights(COS)
+        for i in range(1, ROUNDS):
+            load_frames(i)
+        load_weights(SIN)
+
+        def operand(name):
+            return {
+                "codes": keep.tile([P, N_TILE], U32, name=name + "_codes", align_bytes=64),
+                "scales": keep.tile([P, N_TILE], U8, name=name + "_scales", align_bytes=64),
+            }
+
+        frames_q = [operand("frames%d" % i) for i in range(ROUNDS)]
+        weights_q = {
+            (half, j, g): operand("w%d_%d_%d" % (half, j, g))
+            for half in (COS, SIN)
+            for j in range(COL_TILES)
+            for g in range(PASSES)
+        }
+
+        def transpose_bank(blocks):
+            bank = psum_t.tile([P, len(blocks), P], F32)
+            for s, block in enumerate(blocks):
+                nc.tensor.transpose(bank[:, s, :], block, ident[:])
+            return bank
+
+        def regroup_frames(i):
+            words = x_raw[i][:].bitcast(F32)
+            grouped = stage.tile([P, PAIR * N_FFT], BF16, align_bytes=64)
+            slots = grouped[:].bitcast(F32).rearrange(
+                "p (b g t u) -> p b g t u", b=PAIR, g=PASSES, u=PLANES
+            )
+            for b, copy in enumerate((nc.vector.tensor_copy, nc.scalar.copy)):
+                bank = transpose_bank(
+                    [
+                        words[:, b, WORDS * g + u : WORDS * (g + 1) : PLANES]
+                        for g in range(PASSES)
+                        for u in range(PLANES)
+                    ]
+                )
+                copy(out=slots[:, b, :, :, :], in_=bank[:].rearrange("p (g u) t -> p g t u", u=PLANES))
+            return [(grouped[:], frames_q[i]["codes"][:], frames_q[i]["scales"][:])]
+
+        def regroup_weights(half, c):
+            words = w_raw[(half, c)][:].bitcast(F32)
+            grouped = stage.tile([P, PASSES * W_ROWS * PACK], BF16, align_bytes=64)
+            slots = grouped[:].bitcast(F32).rearrange(
+                "p (g q r u) -> p g q r u", g=PASSES, r=PAIR, u=PLANES
+            )
+            j, part = divmod(c, N_TILE // W_ROWS)
+            columns = slice(W_ROWS * part, W_ROWS * (part + 1))
+            jobs = []
+            for g, copy in enumerate((nc.vector.tensor_copy, nc.scalar.copy)):
+                bank = transpose_bank(
+                    [
+                        words[:, r, WORDS * g + u : WORDS * (g + 1) : PLANES]
+                        for r in range(PAIR)
+                        for u in range(PLANES)
+                    ]
+                )
+                copy(out=slots[:, g, :, :, :], in_=bank[:].rearrange("p (r u) q -> p q r u", u=PLANES))
+                jobs.append(
+                    (
+                        grouped[:, W_ROWS * PACK * g : W_ROWS * PACK * (g + 1)],
+                        weights_q[(half, j, g)]["codes"][:, columns],
+                        weights_q[(half, j, g)]["scales"][:, columns],
+                    )
+                )
+            return jobs
+
+        def quantise(jobs):
+            for values, codes, scales in jobs:
+                nc.vector.quantize_mx(out=codes.bitcast(FP8X4), scales=scales, in_=values)
+
+        def product(half, i, member, j, staged, turn):
+            acc = psum_acc.tile([P, N_TILE], F32)
+            for g in range(PASSES):
+                first = (member * PASSES + g) * P
+                nc.tensor.matmul_mx(
+                    out=acc[:],
+                    lhsT=frames_q[i]["codes"][:, first : first + P].bitcast(FP8X4),
+                    lhsT_scale=frames_q[i]["scales"][:, first : first + P],
+                    rhs=weights_q[(half, j, g)]["codes"][:].bitcast(FP8X4),
+                    rhs_scale=weights_q[(half, j, g)]["scales"][:],
+                    start=(g == 0),
+                    stop=(g == PASSES - 1),
+                )
+            target = staged[:, member, N_TILE * j : N_TILE * (j + 1)]
+            if turn == 0:
+                nc.scalar.mul(out=target, in_=acc[:], mul=signs[half])
+            else:
+                nc.vector.tensor_scalar_mul(out=target, in0=acc[:], scalar1=signs[half])
+
+        def store(half, i, staged, member, count):
+            first = PAIR * i + member
+            nc.sync.dma_start(
+                out=outputs[half][:, first : first + count, :],
+                in_=staged[:, member : member + count, :],
+            )
+
+        waiting = regroup_frames(0)
+        for c in range(W_CHUNKS):
+            regrouped = regroup_weights(COS, c)
+            quantise(waiting)
+            waiting = regrouped
+        quantise(waiting)
+
+        for i in range(ROUNDS):
+            ahead = []
+            if i + 1 < ROUNDS:
+                ahead += regroup_frames(i + 1)
+            if i >= ROUNDS - W_CHUNKS:
+                ahead += regroup_weights(SIN, i - (ROUNDS - W_CHUNKS))
+            staged = results.tile([P, PAIR, N_FFT], F32)
+            for j in range(COL_TILES):
+                for member in range(PAIR):
+                    product(COS, i, member, j, staged, turn=member)
+                if j == 0:
+                    quantise(ahead)
+            store(COS, i, staged, 0, PAIR)
+
+        for i in range(ROUNDS):
+            staged = results.tile([P, PAIR, N_FFT], F32)
+            for member in range(PAIR):
+                for j in range(COL_TILES):
+                    product(SIN, i, member, j, staged, turn=j)
+                if i == ROUNDS - 1:
+                    store(SIN, i, staged, member, 1)
+            if i < ROUNDS - 1:
+                store(SIN, i, staged, 0, PAIR)

@@ -42,6 +42,7 @@ def tile_dftlayer_kernel(tc, x, wsin, wcos, out_0, out_1):
         keep = ctx.enter_context(tc.tile_pool(name="keep", bufs=1))
         stage = ctx.enter_context(tc.tile_pool(name="stage", bufs=4))
         results = ctx.enter_context(tc.tile_pool(name="results", bufs=8))
+        ordered_pool = ctx.enter_context(tc.tile_pool(name="ordered", bufs=3))
         psum_t = ctx.enter_context(tc.psum_pool(name="psum_t", bufs=4))
         psum_acc = ctx.enter_context(tc.psum_pool(name="psum_acc", bufs=4))
 
@@ -90,7 +91,17 @@ def tile_dftlayer_kernel(tc, x, wsin, wcos, out_0, out_1):
                 nc.tensor.transpose(bank[:, s, :], block, ident[:])
             return bank
 
-        def regroup_frames(i):
+        def order_words(i):
+            ordered = ordered_pool.tile([P, PAIR, PASSES, PLANES, P], F32)
+            nc.scalar.copy(
+                out=ordered[:].rearrange("p b g u k -> p (b g) u k"),
+                in_=x_raw[i][:].rearrange("p b n -> p (b n)").bitcast(F32).rearrange(
+                    "p (h k u) -> p h u k", h=PAIR * PASSES, u=PLANES
+                ),
+            )
+            return ordered
+
+        def regroup_frames(i, ordered):
             words = x_raw[i][:].bitcast(F32)
             grouped = stage.tile([P, PAIR * N_FFT], BF16, align_bytes=64)
             slots = grouped[:].bitcast(F32).rearrange(
@@ -100,6 +111,8 @@ def tile_dftlayer_kernel(tc, x, wsin, wcos, out_0, out_1):
                 bank = transpose_bank(
                     [
                         words[:, b, WORDS * g + u : WORDS * (g + 1) : PLANES]
+                        if ordered is None
+                        else ordered[:, b, g, u, :]
                         for g in range(PASSES)
                         for u in range(PLANES)
                     ]
@@ -164,17 +177,18 @@ def tile_dftlayer_kernel(tc, x, wsin, wcos, out_0, out_1):
                 in_=staged[:, member : member + count, :],
             )
 
-        waiting = regroup_frames(0)
+        waiting = regroup_frames(0, None)
         for c in range(W_CHUNKS):
             regrouped = regroup_weights(COS, c)
             quantise(waiting)
             waiting = regrouped
         quantise(waiting)
+        ordered = order_words(1)
 
         for i in range(ROUNDS):
             ahead = []
             if i + 1 < ROUNDS:
-                ahead += regroup_frames(i + 1)
+                ahead += regroup_frames(i + 1, ordered)
             if i >= ROUNDS - W_CHUNKS:
                 ahead += regroup_weights(SIN, i - (ROUNDS - W_CHUNKS))
             staged = results.tile([P, PAIR, N_FFT], F32)
@@ -183,6 +197,8 @@ def tile_dftlayer_kernel(tc, x, wsin, wcos, out_0, out_1):
                     product(COS, i, member, j, staged, turn=member)
                 if j == 0:
                     quantise(ahead)
+                    if i + 2 < ROUNDS:
+                        ordered = order_words(i + 2)
             store(COS, i, staged, 0, PAIR)
 
         for i in range(ROUNDS):

@@ -60,16 +60,17 @@ def tile_dftlayer_kernel(tc, x, wsin, wcos, out_0, out_1):
         def load_frames(i):
             nc.sync.dma_start(out=x_raw[i][:], in_=x_frames[:, PAIR * i : PAIR * (i + 1), 0:N_FFT])
 
-        def load_weights(half):
+        def load_weights(half, c):
             rows = weights[half].rearrange("(c q r) n -> c q r n", q=P, r=PAIR)
-            for c in range(W_CHUNKS):
-                nc.sync.dma_start(out=w_raw[(half, c)][:], in_=rows[c, :, :, :])
+            nc.sync.dma_start(out=w_raw[(half, c)][:], in_=rows[c, :, :, :])
 
         load_frames(0)
-        load_weights(COS)
+        for c in range(W_CHUNKS):
+            load_weights(COS, c)
         for i in range(1, ROUNDS):
             load_frames(i)
-        load_weights(SIN)
+            if i <= W_CHUNKS:
+                load_weights(SIN, i - 1)
 
         def operand(name):
             return {
@@ -91,15 +92,13 @@ def tile_dftlayer_kernel(tc, x, wsin, wcos, out_0, out_1):
                 nc.tensor.transpose(bank[:, s, :], block, ident[:])
             return bank
 
-        def order_words(i):
-            ordered = ordered_pool.tile([P, PAIR, PASSES, PLANES, P], F32)
+        def order_words(i, ordered, b):
             nc.scalar.copy(
-                out=ordered[:].rearrange("p b g u k -> p (b g) u k"),
-                in_=x_raw[i][:].rearrange("p b n -> p (b n)").bitcast(F32).rearrange(
-                    "p (h k u) -> p h u k", h=PAIR * PASSES, u=PLANES
+                out=ordered[:, b, :, :, :],
+                in_=x_raw[i][:, b, :].bitcast(F32).rearrange(
+                    "p (g k u) -> p g u k", g=PASSES, u=PLANES
                 ),
             )
-            return ordered
 
         def regroup_frames(i, ordered):
             words = x_raw[i][:].bitcast(F32)
@@ -183,30 +182,40 @@ def tile_dftlayer_kernel(tc, x, wsin, wcos, out_0, out_1):
             quantise(waiting)
             waiting = regrouped
         quantise(waiting)
-        ordered = order_words(1)
 
-        for i in range(ROUNDS):
+        def new_ordered():
+            tile = ordered_pool.tile([P, PAIR, PASSES, PLANES, P], F32, name="ordered")
+            return tile
+
+        ordered = {1: new_ordered()}
+        for b in range(PAIR):
+            order_words(1, ordered[1], b)
+        for s in range(ROUNDS + W_CHUNKS):
             ahead = []
-            if i + 1 < ROUNDS:
-                ahead += regroup_frames(i + 1, ordered)
-            if i >= ROUNDS - W_CHUNKS:
-                ahead += regroup_weights(SIN, i - (ROUNDS - W_CHUNKS))
-            staged = results.tile([P, PAIR, N_FFT], F32)
-            for j in range(COL_TILES):
-                for member in range(PAIR):
-                    product(COS, i, member, j, staged, turn=member)
-                if j == 0:
-                    quantise(ahead)
-                    if i + 2 < ROUNDS:
-                        ordered = order_words(i + 2)
-            store(COS, i, staged, 0, PAIR)
-
-        for i in range(ROUNDS):
-            staged = results.tile([P, PAIR, N_FFT], F32)
-            for member in range(PAIR):
+            if s + 1 < ROUNDS:
+                ahead += regroup_frames(s + 1, ordered[s + 1])
+            if s < W_CHUNKS:
+                ahead += regroup_weights(SIN, s)
+            if s + 2 < ROUNDS:
+                ordered[s + 2] = new_ordered()
+            if s < ROUNDS:
+                staged = results.tile([P, PAIR, N_FFT], F32)
                 for j in range(COL_TILES):
-                    product(SIN, i, member, j, staged, turn=j)
-                if i == ROUNDS - 1:
-                    store(SIN, i, staged, member, 1)
-            if i < ROUNDS - 1:
-                store(SIN, i, staged, 0, PAIR)
+                    for member in range(PAIR):
+                        product(COS, s, member, j, staged, turn=member)
+                    if j == 0:
+                        quantise(ahead)
+                    if s + 2 < ROUNDS:
+                        order_words(s + 2, ordered[s + 2], j)
+                store(COS, s, staged, 0, PAIR)
+            i = s - W_CHUNKS
+            if i >= 0:
+                last = i == ROUNDS - 1
+                staged = results.tile([P, PAIR, N_FFT], F32)
+                for member in range(PAIR):
+                    for j in range(COL_TILES):
+                        product(SIN, i, member, j, staged, turn=j)
+                    if last:
+                        store(SIN, i, staged, member, 1)
+                if not last:
+                    store(SIN, i, staged, 0, PAIR)

@@ -42,7 +42,7 @@ def tile_dftlayer_kernel(tc, x, wsin, wcos, out_0, out_1):
         keep = ctx.enter_context(tc.tile_pool(name="keep", bufs=1))
         stage = ctx.enter_context(tc.tile_pool(name="stage", bufs=4))
         results = ctx.enter_context(tc.tile_pool(name="results", bufs=8))
-        ordered_pool = ctx.enter_context(tc.tile_pool(name="ordered", bufs=3))
+        ordered_pool = ctx.enter_context(tc.tile_pool(name="ordered", bufs=4))
         psum_t = ctx.enter_context(tc.psum_pool(name="psum_t", bufs=4))
         psum_acc = ctx.enter_context(tc.psum_pool(name="psum_acc", bufs=4))
 
@@ -67,10 +67,10 @@ def tile_dftlayer_kernel(tc, x, wsin, wcos, out_0, out_1):
         load_frames(0)
         for c in range(W_CHUNKS):
             load_weights(COS, c)
+        for c in range(W_CHUNKS):
+            load_weights(SIN, c)
         for i in range(1, ROUNDS):
             load_frames(i)
-            if i <= W_CHUNKS:
-                load_weights(SIN, i - 1)
 
         def operand(name):
             return {
@@ -92,35 +92,36 @@ def tile_dftlayer_kernel(tc, x, wsin, wcos, out_0, out_1):
                 nc.tensor.transpose(bank[:, s, :], block, ident[:])
             return bank
 
-        def order_words(i, ordered, b):
-            nc.scalar.copy(
-                out=ordered[:, b, :, :, :],
-                in_=x_raw[i][:, b, :].bitcast(F32).rearrange(
-                    "p (g k u) -> p g u k", g=PASSES, u=PLANES
-                ),
-            )
+        def order_words(raw):
+            ordered = ordered_pool.tile([P, PAIR, PASSES, PLANES, P], F32)
+            for b, copy in enumerate((nc.vector.tensor_copy, nc.scalar.copy)):
+                copy(
+                    out=ordered[:, b, :, :, :],
+                    in_=raw[:, b, :].bitcast(F32).rearrange(
+                        "p (g k u) -> p g u k", g=PASSES, u=PLANES
+                    ),
+                )
+            return ordered
+
+        def words_of(raw, ordered):
+            if ordered is not None:
+                return lambda b, g, u: ordered[:, b, g, u, :]
+            words = raw[:].bitcast(F32)
+            return lambda b, g, u: words[:, b, WORDS * g + u : WORDS * (g + 1) : PLANES]
 
         def regroup_frames(i, ordered):
-            words = x_raw[i][:].bitcast(F32)
+            block = words_of(x_raw[i], ordered)
             grouped = stage.tile([P, PAIR * N_FFT], BF16, align_bytes=64)
             slots = grouped[:].bitcast(F32).rearrange(
                 "p (b g t u) -> p b g t u", b=PAIR, g=PASSES, u=PLANES
             )
             for b, copy in enumerate((nc.vector.tensor_copy, nc.scalar.copy)):
-                bank = transpose_bank(
-                    [
-                        words[:, b, WORDS * g + u : WORDS * (g + 1) : PLANES]
-                        if ordered is None
-                        else ordered[:, b, g, u, :]
-                        for g in range(PASSES)
-                        for u in range(PLANES)
-                    ]
-                )
+                bank = transpose_bank([block(b, g, u) for g in range(PASSES) for u in range(PLANES)])
                 copy(out=slots[:, b, :, :, :], in_=bank[:].rearrange("p (g u) t -> p g t u", u=PLANES))
             return [(grouped[:], frames_q[i]["codes"][:], frames_q[i]["scales"][:])]
 
-        def regroup_weights(half, c):
-            words = w_raw[(half, c)][:].bitcast(F32)
+        def regroup_weights(half, c, ordered):
+            block = words_of(w_raw[(half, c)], ordered)
             grouped = stage.tile([P, PASSES * W_ROWS * PACK], BF16, align_bytes=64)
             slots = grouped[:].bitcast(F32).rearrange(
                 "p (g q r u) -> p g q r u", g=PASSES, r=PAIR, u=PLANES
@@ -129,13 +130,7 @@ def tile_dftlayer_kernel(tc, x, wsin, wcos, out_0, out_1):
             columns = slice(W_ROWS * part, W_ROWS * (part + 1))
             jobs = []
             for g, copy in enumerate((nc.vector.tensor_copy, nc.scalar.copy)):
-                bank = transpose_bank(
-                    [
-                        words[:, r, WORDS * g + u : WORDS * (g + 1) : PLANES]
-                        for r in range(PAIR)
-                        for u in range(PLANES)
-                    ]
-                )
+                bank = transpose_bank([block(r, g, u) for r in range(PAIR) for u in range(PLANES)])
                 copy(out=slots[:, g, :, :, :], in_=bank[:].rearrange("p (r u) q -> p q r u", u=PLANES))
                 jobs.append(
                     (
@@ -176,46 +171,78 @@ def tile_dftlayer_kernel(tc, x, wsin, wcos, out_0, out_1):
                 in_=staged[:, member : member + count, :],
             )
 
-        waiting = regroup_frames(0, None)
+        ordered = {}
+        waiting = []
+
+        def order(*unit):
+            raw = x_raw[unit[0]] if len(unit) == 1 else w_raw[unit]
+            ordered[unit] = order_words(raw)
+
+        def regroup(*unit):
+            if len(unit) == 1:
+                waiting.append(regroup_frames(unit[0], ordered.get(unit)))
+            else:
+                waiting.append(regroup_weights(unit[0], unit[1], ordered.get(unit)))
+
+        def quantise_next():
+            quantise(waiting.pop(0))
+
+        def quantise_all():
+            while waiting:
+                quantise_next()
+
+        staged = {}
+
+        def columns_of(half, i, j):
+            if j == 0:
+                staged[half, i] = results.tile([P, PAIR, N_FFT], F32, name="staged")
+            for member in range(PAIR):
+                product(half, i, member, j, staged[half, i], turn=member)
+            if j == COL_TILES - 1:
+                store(half, i, staged[half, i], 0, PAIR)
+
+        def signal_of(half, i, member):
+            if member == 0:
+                staged[half, i] = results.tile([P, PAIR, N_FFT], F32, name="staged")
+            for j in range(COL_TILES):
+                product(half, i, member, j, staged[half, i], turn=j)
+            store(half, i, staged[half, i], member, 1)
+
+        regroup(0)
         for c in range(W_CHUNKS):
-            regrouped = regroup_weights(COS, c)
-            quantise(waiting)
-            waiting = regrouped
-        quantise(waiting)
-
-        def new_ordered():
-            tile = ordered_pool.tile([P, PAIR, PASSES, PLANES, P], F32, name="ordered")
-            return tile
-
-        ordered = {1: new_ordered()}
-        for b in range(PAIR):
-            order_words(1, ordered[1], b)
-        for s in range(ROUNDS + W_CHUNKS):
-            ahead = []
-            if s + 1 < ROUNDS:
-                ahead += regroup_frames(s + 1, ordered[s + 1])
-            if s < W_CHUNKS:
-                ahead += regroup_weights(SIN, s)
-            if s + 2 < ROUNDS:
-                ordered[s + 2] = new_ordered()
-            if s < ROUNDS:
-                staged = results.tile([P, PAIR, N_FFT], F32)
-                for j in range(COL_TILES):
-                    for member in range(PAIR):
-                        product(COS, s, member, j, staged, turn=member)
-                    if j == 0:
-                        quantise(ahead)
-                    if s + 2 < ROUNDS:
-                        order_words(s + 2, ordered[s + 2], j)
-                store(COS, s, staged, 0, PAIR)
-            i = s - W_CHUNKS
-            if i >= 0:
-                last = i == ROUNDS - 1
-                staged = results.tile([P, PAIR, N_FFT], F32)
-                for member in range(PAIR):
-                    for j in range(COL_TILES):
-                        product(SIN, i, member, j, staged, turn=j)
-                    if last:
-                        store(SIN, i, staged, member, 1)
-                if not last:
-                    store(SIN, i, staged, 0, PAIR)
+            regroup(COS, c)
+            quantise_next()
+        quantise_all()
+        columns_of(COS, 0, 0)
+        regroup(SIN, 0)
+        order(SIN, 2)
+        regroup(SIN, 1)
+        quantise_all()
+        columns_of(COS, 0, 1)
+        order(SIN, 3)
+        regroup(SIN, 2)
+        order(1)
+        regroup(SIN, 3)
+        quantise_all()
+        order(2)
+        regroup(1)
+        quantise_all()
+        columns_of(SIN, 0, 0)
+        columns_of(SIN, 0, 1)
+        order(3)
+        regroup(2)
+        for i in range(1, ROUNDS):
+            signal_of(COS, i, 0)
+            if i == 1:
+                quantise_all()
+                regroup(3)
+            signal_of(COS, i, 1)
+            if i == 1:
+                quantise_all()
+            elif i + 2 < ROUNDS:
+                regroup(i + 2)
+            signal_of(SIN, i, 0)
+            quantise_all()
+            if i + 3 < ROUNDS:
+                order(i + 3)
+            signal_of(SIN, i, 1)

@@ -46,6 +46,12 @@ def tile_dftlayer_kernel(tc, x, wsin, wcos, out_0, out_1):
         psum_t = ctx.enter_context(tc.psum_pool(name="psum_t", bufs=4))
         psum_acc = ctx.enter_context(tc.psum_pool(name="psum_acc", bufs=4))
 
+        zeros = keep.tile([P, N_TILE], BF16, name="zeros")
+        nc.vector.memset(zeros[:], 0.0)
+        acc = psum_acc.tile([P, N_TILE], F32, name="acc")
+        for k in range(4):
+            nc.tensor.matmul(acc[:], lhsT=zeros[:, 0:P], rhs=zeros[:], start=True, stop=True)
+
         ident = keep.tile([P, P], F32, name="ident")
         make_identity(nc, ident[:])
 
@@ -110,12 +116,13 @@ def tile_dftlayer_kernel(tc, x, wsin, wcos, out_0, out_1):
             return lambda b, g, u: words[:, b, WORDS * g + u : WORDS * (g + 1) : PLANES]
 
         def regroup_frames(i, ordered):
+            copies = (nc.scalar.copy if i == 1 else nc.vector.tensor_copy, nc.scalar.copy)
             block = words_of(x_raw[i], ordered)
             grouped = stage.tile([P, PAIR * N_FFT], BF16, align_bytes=64)
             slots = grouped[:].bitcast(F32).rearrange(
                 "p (b g t u) -> p b g t u", b=PAIR, g=PASSES, u=PLANES
             )
-            for b, copy in enumerate((nc.vector.tensor_copy, nc.scalar.copy)):
+            for b, copy in enumerate(copies):
                 bank = transpose_bank([block(b, g, u) for g in range(PASSES) for u in range(PLANES)])
                 copy(out=slots[:, b, :, :, :], in_=bank[:].rearrange("p (g u) t -> p g t u", u=PLANES))
             return [(grouped[:], frames_q[i]["codes"][:], frames_q[i]["scales"][:])]
@@ -193,53 +200,54 @@ def tile_dftlayer_kernel(tc, x, wsin, wcos, out_0, out_1):
 
         staged = {}
 
-        def columns_of(half, i, j):
-            if j == 0:
+        def part_of(half, i, member, j):
+            if (half, i) not in staged:
                 staged[half, i] = results.tile([P, PAIR, N_FFT], F32, name="staged")
-            for member in range(PAIR):
-                product(half, i, member, j, staged[half, i], turn=member)
-            if j == COL_TILES - 1:
-                store(half, i, staged[half, i], 0, PAIR)
+            product(half, i, member, j, staged[half, i], turn=(member + j) % 2)
 
         def signal_of(half, i, member):
-            if member == 0:
-                staged[half, i] = results.tile([P, PAIR, N_FFT], F32, name="staged")
             for j in range(COL_TILES):
-                product(half, i, member, j, staged[half, i], turn=j)
+                part_of(half, i, member, j)
             store(half, i, staged[half, i], member, 1)
 
         regroup(0)
-        for c in range(W_CHUNKS):
-            regroup(COS, c)
-            quantise_next()
+        regroup(COS, 0)
+        quantise_next()
+        regroup(COS, 1)
         quantise_all()
-        columns_of(COS, 0, 0)
+        regroup(COS, 2)
+        regroup(COS, 3)
+        quantise_next()
         regroup(SIN, 0)
+        quantise_next()
         order(SIN, 2)
-        regroup(SIN, 1)
-        quantise_all()
-        columns_of(COS, 0, 1)
+        part_of(COS, 0, 0, 0)
+        part_of(COS, 0, 1, 0)
         order(SIN, 3)
-        regroup(SIN, 2)
+        regroup(SIN, 1)
         order(1)
+        quantise_all()
+        part_of(COS, 0, 0, 1)
+        regroup(SIN, 2)
         regroup(SIN, 3)
         quantise_all()
+        part_of(COS, 0, 1, 1)
+        store(COS, 0, staged[COS, 0], 0, PAIR)
+        part_of(SIN, 0, 0, 0)
         order(2)
         regroup(1)
+        part_of(SIN, 0, 1, 0)
         quantise_all()
-        columns_of(SIN, 0, 0)
-        columns_of(SIN, 0, 1)
         order(3)
+        part_of(SIN, 0, 0, 1)
+        part_of(SIN, 0, 1, 1)
+        store(SIN, 0, staged[SIN, 0], 0, PAIR)
         regroup(2)
         for i in range(1, ROUNDS):
             signal_of(COS, i, 0)
-            if i == 1:
-                quantise_all()
-                regroup(3)
+            quantise_all()
             signal_of(COS, i, 1)
-            if i == 1:
-                quantise_all()
-            elif i + 2 < ROUNDS:
+            if i + 2 < ROUNDS:
                 regroup(i + 2)
             signal_of(SIN, i, 0)
             quantise_all()

from contextlib import ExitStack

import concourse.mybir as mybir
from concourse.masks import make_identity

BF16 = mybir.dt.bfloat16
F32 = mybir.dt.float32
U32 = mybir.dt.uint32
U8 = mybir.dt.uint8
FP8X4 = mybir.dt.float8_e4m3fn_x4

P = 128
N_FFT = 1024
SIGNALS = 16
FRAMES = 128
STRIDE = N_FFT + 1
PACK = 4
K_PASS = P * PACK
PASSES = N_FFT // K_PASS
PLANES = 2
WORDS = K_PASS // 2
N_TILE = 512
COL_TILES = N_FFT // N_TILE
PAIR = 2
ROUNDS = SIGNALS // PAIR
W_ROWS = PAIR * P
W_CHUNKS = N_FFT // W_ROWS
COS = 0
SIN = 1

FLOPS = 2 * 2 * SIGNALS * FRAMES * N_FFT * N_FFT


def tile_dftlayer_kernel(tc, x, wsin, wcos, out_0, out_1):
    nc = tc.nc
    weights = {COS: wcos, SIN: wsin}
    outputs = {COS: out_0, SIN: out_1}
    signs = {COS: 1.0, SIN: -1.0}

    with ExitStack() as ctx:
        ctx.enter_context(tc.manual_schedule())
        keep = ctx.enter_context(tc.tile_pool(name="keep", bufs=1))
        stage = ctx.enter_context(tc.tile_pool(name="stage", bufs=4))
        results = ctx.enter_context(tc.tile_pool(name="results", bufs=8))
        ordered_pool = ctx.enter_context(tc.tile_pool(name="ordered", bufs=4))
        psum_t = ctx.enter_context(tc.psum_pool(name="psum_t", bufs=4))
        psum_acc = ctx.enter_context(tc.psum_pool(name="psum_acc", bufs=4))

        zeros = keep.tile([P, N_TILE], BF16, name="zeros")
        nc.vector.memset(zeros[:], 0.0)
        acc = psum_acc.tile([P, N_TILE], F32, name="acc")
        for k in range(4):
            nc.tensor.matmul(acc[:], lhsT=zeros[:, 0:P], rhs=zeros[:], start=True, stop=True)

        ident = keep.tile([P, P], F32, name="ident")
        make_identity(nc, ident[:])

        x_frames = x.rearrange("o b (t s) -> t (o b) s", s=STRIDE)
        x_raw = [keep.tile([P, PAIR, N_FFT], BF16, name="x_raw%d" % i) for i in range(ROUNDS)]
        w_raw = {
            (half, c): keep.tile([P, PAIR, N_FFT], BF16, name="w_raw%d_%d" % (half, c))
            for half in (COS, SIN)
            for c in range(W_CHUNKS)
        }

        def load_frames(i):
            nc.sync.dma_start(out=x_raw[i][:], in_=x_frames[:, PAIR * i : PAIR * (i + 1), 0:N_FFT])

        def load_weights(half, c):
            rows = weights[half].rearrange("(c q r) n -> c q r n", q=P, r=PAIR)
            nc.sync.dma_start(out=w_raw[(half, c)][:], in_=rows[c, :, :, :])

        load_frames(0)
        for c in range(W_CHUNKS):
            load_weights(COS, c)
        for c in range(W_CHUNKS):
            load_weights(SIN, c)
        for i in range(1, ROUNDS):
            load_frames(i)

        def operand(name):
            return {
                "codes": keep.tile([P, N_TILE], U32, name=name + "_codes", align_bytes=64),
                "scales": keep.tile([P, N_TILE], U8, name=name + "_scales", align_bytes=64),
            }

        frames_q = [operand("frames%d" % i) for i in range(ROUNDS)]
        weights_q = {
            (half, j, g): operand("w%d_%d_%d" % (half, j, g))
            for half in (COS, SIN)
            for j in range(COL_TILES)
            for g in range(PASSES)
        }

        def transpose_bank(blocks):
            bank = psum_t.tile([P, len(blocks), P], F32)
            for s, block in enumerate(blocks):
                nc.tensor.transpose(bank[:, s, :], block, ident[:])
            return bank

        def order_words(raw):
            ordered = ordered_pool.tile([P, PAIR, PASSES, PLANES, P], F32)
            for b, copy in enumerate((nc.vector.tensor_copy, nc.scalar.copy)):
                copy(
                    out=ordered[:, b, :, :, :],
                    in_=raw[:, b, :].bitcast(F32).rearrange(
                        "p (g k u) -> p g u k", g=PASSES, u=PLANES
                    ),
                )
            return ordered

        def words_of(raw, ordered):
            if ordered is not None:
                return lambda b, g, u: ordered[:, b, g, u, :]
            words = raw[:].bitcast(F32)
            return lambda b, g, u: words[:, b, WORDS * g + u : WORDS * (g + 1) : PLANES]

        def regroup_frames(i, ordered):
            copies = (nc.scalar.copy if i == 1 else nc.vector.tensor_copy, nc.scalar.copy)
            block = words_of(x_raw[i], ordered)
            grouped = stage.tile([P, PAIR * N_FFT], BF16, align_bytes=64)
            slots = grouped[:].bitcast(F32).rearrange(
                "p (b g t u) -> p b g t u", b=PAIR, g=PASSES, u=PLANES
            )
            for b, copy in enumerate(copies):
                bank = transpose_bank([block(b, g, u) for g in range(PASSES) for u in range(PLANES)])
                copy(out=slots[:, b, :, :, :], in_=bank[:].rearrange("p (g u) t -> p g t u", u=PLANES))
            return [(grouped[:], frames_q[i]["codes"][:], frames_q[i]["scales"][:])]

        def regroup_weights(half, c, ordered):
            block = words_of(w_raw[(half, c)], ordered)
            grouped = stage.tile([P, PASSES * W_ROWS * PACK], BF16, align_bytes=64)
            slots = grouped[:].bitcast(F32).rearrange(
                "p (g q r u) -> p g q r u", g=PASSES, r=PAIR, u=PLANES
            )
            j, part = divmod(c, N_TILE // W_ROWS)
            columns = slice(W_ROWS * part, W_ROWS * (part + 1))
            jobs = []
            for g, copy in enumerate((nc.vector.tensor_copy, nc.scalar.copy)):
                bank = transpose_bank([block(r, g, u) for r in range(PAIR) for u in range(PLANES)])
                copy(out=slots[:, g, :, :, :], in_=bank[:].rearrange("p (r u) q -> p q r u", u=PLANES))
                jobs.append(
                    (
                        grouped[:, W_ROWS * PACK * g : W_ROWS * PACK * (g + 1)],
                        weights_q[(half, j, g)]["codes"][:, columns],
                        weights_q[(half, j, g)]["scales"][:, columns],
                    )
                )
            return jobs

        def quantise(jobs):
            for values, codes, scales in jobs:
                nc.vector.quantize_mx(out=codes.bitcast(FP8X4), scales=scales, in_=values)

        def product(half, i, member, j, staged, turn):
            acc = psum_acc.tile([P, N_TILE], F32)
            for g in range(PASSES):
                first = (member * PASSES + g) * P
                nc.tensor.matmul_mx(
                    out=acc[:],
                    lhsT=frames_q[i]["codes"][:, first : first + P].bitcast(FP8X4),
                    lhsT_scale=frames_q[i]["scales"][:, first : first + P],
                    rhs=weights_q[(half, j, g)]["codes"][:].bitcast(FP8X4),
                    rhs_scale=weights_q[(half, j, g)]["scales"][:],
                    start=(g == 0),
                    stop=(g == PASSES - 1),
                )
            target = staged[:, member, N_TILE * j : N_TILE * (j + 1)]
            if turn == 0:
                nc.scalar.mul(out=target, in_=acc[:], mul=signs[half])
            else:
                nc.vector.tensor_scalar_mul(out=target, in0=acc[:], scalar1=signs[half])

        def store(half, i, staged, member, count):
            first = PAIR * i + member
            nc.sync.dma_start(
                out=outputs[half][:, first : first + count, :],
                in_=staged[:, member : member + count, :],
            )

        ordered = {}
        waiting = []

        def order(*unit):
            raw = x_raw[unit[0]] if len(unit) == 1 else w_raw[unit]
            ordered[unit] = order_words(raw)

        def regroup(*unit):
            if len(unit) == 1:
                waiting.append(regroup_frames(unit[0], ordered.get(unit)))
            else:
                waiting.append(regroup_weights(unit[0], unit[1], ordered.get(unit)))

        def quantise_next():
            quantise(waiting.pop(0))

        def quantise_all():
            while waiting:
                quantise_next()

        staged = {}

        def part_of(half, i, member, j):
            if (half, i) not in staged:
                staged[half, i] = results.tile([P, PAIR, N_FFT], F32, name="staged")
            product(half, i, member, j, staged[half, i], turn=(member + j) % 2)

        def signal_of(half, i, member):
            for j in range(COL_TILES):
                part_of(half, i, member, j)
            store(half, i, staged[half, i], member, 1)

        regroup(0)
        regroup(COS, 0)
        quantise_next()
        regroup(COS, 1)
        quantise_all()
        regroup(COS, 2)
        regroup(COS, 3)
        quantise_next()
        regroup(SIN, 0)
        quantise_next()
        order(SIN, 2)
        part_of(COS, 0, 0, 0)
        part_of(COS, 0, 1, 0)
        order(SIN, 3)
        regroup(SIN, 1)
        order(1)
        quantise_all()
        part_of(COS, 0, 0, 1)
        regroup(SIN, 2)
        regroup(SIN, 3)
        quantise_all()
        part_of(COS, 0, 1, 1)
        store(COS, 0, staged[COS, 0], 0, PAIR)
        part_of(SIN, 0, 0, 0)
        order(2)
        regroup(1)
        part_of(SIN, 0, 1, 0)
        quantise_all()
        order(3)
        part_of(SIN, 0, 0, 1)
        part_of(SIN, 0, 1, 1)
        store(SIN, 0, staged[SIN, 0], 0, PAIR)
        regroup(2)
        for i in range(1, ROUNDS):
            signal_of(COS, i, 0)
            quantise_all()
            signal_of(COS, i, 1)
            if i + 2 < ROUNDS:
                regroup(i + 2)
            signal_of(SIN, i, 0)
            quantise_all()
            if i + 3 < ROUNDS:
                order(i + 3)
            signal_of(SIN, i, 1)
